import numpy as np
import ml_dtypes

BF16 = ml_dtypes.bfloat16


def bf(x):
    return np.asarray(x, np.float32).astype(BF16)


def f32(x):
    return np.asarray(x, np.float32)


def f64(x):
    return np.asarray(x).astype(np.float64)


def striped(idx):
    return np.tile(idx.reshape(-1, 16).T, (8, 1))


D, S, H, O, N, Q = 128, 2048, 512, 64, 512, 256


def setup_inputs():
    return {"table": bf(np.random.standard_normal((D, S))), "w1": bf(np.random.standard_normal((D, H)) / np.sqrt(D)), "b1": f32(0.2 * np.random.standard_normal((H, 1))), "w2": f32(2.0 * np.random.standard_normal((H, O)) / np.sqrt(O)), "offs": striped(np.random.permutation(np.tile(np.arange(S), 2))[:N])}


def reference(table, w1, b1, w2, offs):
    idx = offs[:16].T.reshape(-1)
    h = np.tanh(f64(w1).T @ f64(table)[:, idx] + f64(b1))
    d = 1.0 - h * h
    c = np.sum(f64(w2) * f64(w2), axis=1, keepdims=True)
    ha, hb = h[:, :Q], h[:, Q:]
    da, db = d[:, :Q], d[:, Q:]
    bias_diag = da * da * c - 2.0 * da * db * c + db * db * c
    w2_diag = (ha - hb) ** 2
    return np.concatenate([bias_diag, w2_diag], axis=1)

@@ -1,0 +1,56 @@
+import concourse.mybir as mybir
+
+P = 128
+D, S, H, O, N, Q = 128, 2048, 512, 64, 512, 256
+T = H // P
+
+FLOPS = 2 * D * H * N
+
+BF16, F32, U16 = mybir.dt.bfloat16, mybir.dt.float32, mybir.dt.uint16
+TANH = mybir.ActivationFunctionType.Tanh
+SQUARE = mybir.ActivationFunctionType.Square
+MULT = mybir.AluOpType.mult
+
+
+def tile_contrastivehessiancalculator_kernel(tc, table, w1, b1, w2, offs, out):
+    nc = tc.nc
+    with (
+        tc.tile_pool(name="held", bufs=1) as held,
+        tc.tile_pool(name="work", bufs=2) as work,
+        tc.psum_pool(name="psum", bufs=T) as psum,
+    ):
+        offsets = held.tile([P, N // 16], U16, name="offsets")
+        nc.sync.dma_start(offsets[:], offs)
+        table_sb = held.tile([P, S], BF16, name="table_sb")
+        nc.sync.dma_start(table_sb[:], table)
+        w1_sb = held.tile([P, H], BF16, name="w1_sb")
+        nc.scalar.dma_start(w1_sb[:], w1)
+        w2_sb = held.tile([P, T, O], F32, name="w2_sb")
+        nc.scalar.dma_start(w2_sb[:], w2.rearrange("(t p) o -> p t o", p=P))
+        b1_sb = held.tile([P, T], F32, name="b1_sb")
+        with nc.allow_non_contiguous_dma(reason="512 biases, one to a partition and block"):
+            nc.gpsimd.dma_start(b1_sb[:], b1.rearrange("(t p) o -> p (t o)", p=P))
+
+        w2_sq = held.tile([P, T, O], F32, name="w2_sq")
+        nc.vector.tensor_mul(w2_sq[:], w2_sb[:], w2_sb[:])
+        c = held.tile([P, T], F32, name="c")
+        nc.vector.reduce_sum(c[:], w2_sq[:], axis=mybir.AxisListType.X)
+
+        for t in range(T):
+            z = psum.tile([P, N], F32, name="z")
+            nc.tensor.matmul(
+                z[:], w1_sb[:, t * P : (t + 1) * P], table_sb[:].indirect(offsets[:]), start=True, stop=True
+            )
+            h = work.tile([P, N], F32, name="h")
+            nc.scalar.activation(h[:], z[:], TANH, bias=b1_sb[:, t : t + 1])
+            anchor, partner = h[:, :Q], h[:, Q:]
+
+            both = work.tile([P, N], F32, name="both")
+            nc.vector.tensor_add(both[:, :Q], anchor, partner)
+            nc.vector.tensor_sub(both[:, Q:], anchor, partner)
+            res = work.tile([P, N], F32, name="res")
+            nc.scalar.activation(res[:], both[:], SQUARE)
+            nc.vector.scalar_tensor_tensor(
+                res[:, :Q], res[:, Q:], c[:, t : t + 1], res[:, :Q], op0=MULT, op1=MULT
+            )
+            nc.sync.dma_start(out[t * P : (t + 1) * P, :], res[:])

@@ -11,46 +11,65 @@ TANH = mybir.ActivationFunctionType.Tanh
 SQUARE = mybir.ActivationFunctionType.Square
 MULT = mybir.AluOpType.mult
 
+WARM = 6
+
 
 def tile_contrastivehessiancalculator_kernel(tc, table, w1, b1, w2, offs, out):
     nc = tc.nc
     with (
         tc.tile_pool(name="held", bufs=1) as held,
-        tc.tile_pool(name="work", bufs=2) as work,
+        tc.tile_pool(name="work", bufs=T) as work,
         tc.psum_pool(name="psum", bufs=T) as psum,
+        tc.psum_pool(name="psum_warm", bufs=1) as psum_warm,
     ):
-        offsets = held.tile([P, N // 16], U16, name="offsets")
-        nc.sync.dma_start(offsets[:], offs)
-        table_sb = held.tile([P, S], BF16, name="table_sb")
-        nc.sync.dma_start(table_sb[:], table)
         w1_sb = held.tile([P, H], BF16, name="w1_sb")
         nc.scalar.dma_start(w1_sb[:], w1)
-        w2_sb = held.tile([P, T, O], F32, name="w2_sb")
-        nc.scalar.dma_start(w2_sb[:], w2.rearrange("(t p) o -> p t o", p=P))
+        table_sb = held.tile([P, S], BF16, name="table_sb")
+        nc.sync.dma_start(table_sb[:, : S // 2], table[:, : S // 2])
+        nc.scalar.dma_start(table_sb[:, S // 2 :], table[:, S // 2 :])
+        offsets = held.tile([P, N // 16], U16, name="offsets")
+        nc.sync.dma_start(offsets[:], offs)
         b1_sb = held.tile([P, T], F32, name="b1_sb")
-        with nc.allow_non_contiguous_dma(reason="512 biases, one to a partition and block"):
-            nc.gpsimd.dma_start(b1_sb[:], b1.rearrange("(t p) o -> p (t o)", p=P))
+        nc.sync.dma_start(b1_sb[:], b1.rearrange("(p t) o -> p (t o)", t=T))
+        w2_sb = held.tile([P, T, O], F32, name="w2_sb")
+        nc.sync.dma_start(w2_sb[:], w2.rearrange("(p t) o -> p t o", t=T))
+        out_blocks = out.rearrange("(p t) n -> p t n", t=T)
+
+        zeros = held.tile([P, N], BF16, name="zeros")
+        nc.vector.memset(zeros[:], 0.0)
+        tanh_of_zero = held.tile([P, 1], F32, name="tanh_of_zero")
+        nc.scalar.activation(tanh_of_zero[:], zeros[:, :1], TANH)
+        warm = psum_warm.tile([P, N], F32, name="warm")
+        for i in range(WARM):
+            nc.tensor.matmul(warm[:], zeros[:, :P], zeros[:], start=True, stop=True)
+
+        w1_blocks = held.tile([P, T, P], BF16, name="w1_blocks")
+        nc.vector.tensor_copy(w1_blocks[:], w1_sb[:].rearrange("k (p t) -> k t p", t=T))
 
         w2_sq = held.tile([P, T, O], F32, name="w2_sq")
         nc.vector.tensor_mul(w2_sq[:], w2_sb[:], w2_sb[:])
         c = held.tile([P, T], F32, name="c")
         nc.vector.reduce_sum(c[:], w2_sq[:], axis=mybir.AxisListType.X)
 
-        for t in range(T):
+        res = held.tile([P, T, N], F32, name="res")
+
+        def sums_and_differences(t):
             z = psum.tile([P, N], F32, name="z")
-            nc.tensor.matmul(
-                z[:], w1_sb[:, t * P : (t + 1) * P], table_sb[:].indirect(offsets[:]), start=True, stop=True
-            )
+            nc.tensor.matmul(z[:], w1_blocks[:, t, :], table_sb[:].indirect(offsets[:]), start=True, stop=True)
             h = work.tile([P, N], F32, name="h")
             nc.scalar.activation(h[:], z[:], TANH, bias=b1_sb[:, t : t + 1])
-            anchor, partner = h[:, :Q], h[:, Q:]
-
             both = work.tile([P, N], F32, name="both")
-            nc.vector.tensor_add(both[:, :Q], anchor, partner)
-            nc.vector.tensor_sub(both[:, Q:], anchor, partner)
-            res = work.tile([P, N], F32, name="res")
-            nc.scalar.activation(res[:], both[:], SQUARE)
+            nc.vector.tensor_add(both[:, :Q], h[:, :Q], h[:, Q:])
+            nc.vector.tensor_sub(both[:, Q:], h[:, :Q], h[:, Q:])
+            return both
+
+        both_next = sums_and_differences(0)
+        for t in range(T):
+            both = both_next
+            if t + 1 < T:
+                both_next = sums_and_differences(t + 1)
+            nc.scalar.activation(res[:, t, :], both[:], SQUARE)
             nc.vector.scalar_tensor_tensor(
-                res[:, :Q], res[:, Q:], c[:, t : t + 1], res[:, :Q], op0=MULT, op1=MULT
+                res[:, t, :Q], res[:, t, Q:], c[:, t : t + 1], res[:, t, :Q], op0=MULT, op1=MULT
             )
-            nc.sync.dma_start(out[t * P : (t + 1) * P, :], res[:])
+            nc.sync.dma_start(out_blocks[:, t, :], res[:, t, :])

@@ -11,8 +11,6 @@ TANH = mybir.ActivationFunctionType.Tanh
 SQUARE = mybir.ActivationFunctionType.Square
 MULT = mybir.AluOpType.mult
 
-WARM = 6
-
 
 def tile_contrastivehessiancalculator_kernel(tc, table, w1, b1, w2, offs, out):
     nc = tc.nc
@@ -20,7 +18,6 @@ def tile_contrastivehessiancalculator_kernel(tc, table, w1, b1, w2, offs, out):
         tc.tile_pool(name="held", bufs=1) as held,
         tc.tile_pool(name="work", bufs=T) as work,
         tc.psum_pool(name="psum", bufs=T) as psum,
-        tc.psum_pool(name="psum_warm", bufs=1) as psum_warm,
     ):
         w1_sb = held.tile([P, H], BF16, name="w1_sb")
         nc.scalar.dma_start(w1_sb[:], w1)
@@ -35,13 +32,10 @@ def tile_contrastivehessiancalculator_kernel(tc, table, w1, b1, w2, offs, out):
         nc.sync.dma_start(w2_sb[:], w2.rearrange("(p t) o -> p t o", t=T))
         out_blocks = out.rearrange("(p t) n -> p t n", t=T)
 
-        zeros = held.tile([P, N], BF16, name="zeros")
-        nc.vector.memset(zeros[:], 0.0)
+        zero = held.tile([P, 1], F32, name="zero")
+        nc.vector.memset(zero[:], 0.0)
         tanh_of_zero = held.tile([P, 1], F32, name="tanh_of_zero")
-        nc.scalar.activation(tanh_of_zero[:], zeros[:, :1], TANH)
-        warm = psum_warm.tile([P, N], F32, name="warm")
-        for i in range(WARM):
-            nc.tensor.matmul(warm[:], zeros[:, :P], zeros[:], start=True, stop=True)
+        nc.scalar.activation(tanh_of_zero[:], zero[:], TANH)
 
         w1_blocks = held.tile([P, T, P], BF16, name="w1_blocks")
         nc.vector.tensor_copy(w1_blocks[:], w1_sb[:].rearrange("k (p t) -> k t p", t=T))

@@ -29,7 +29,7 @@ def tile_contrastivehessiancalculator_kernel(tc, table, w1, b1, w2, offs, out):
         b1_sb = held.tile([P, T], F32, name="b1_sb")
         nc.sync.dma_start(b1_sb[:], b1.rearrange("(p t) o -> p (t o)", t=T))
         w2_sb = held.tile([P, T, O], F32, name="w2_sb")
-        nc.sync.dma_start(w2_sb[:], w2.rearrange("(p t) o -> p t o", t=T))
+        nc.gpsimd.dma_start(w2_sb[:], w2.rearrange("(p t) o -> p t o", t=T))
         out_blocks = out.rearrange("(p t) n -> p t n", t=T)
 
         zero = held.tile([P, 1], F32, name="zero")
@@ -63,7 +63,8 @@ def tile_contrastivehessiancalculator_kernel(tc, table, w1, b1, w2, offs, out):
             if t + 1 < T:
                 both_next = sums_and_differences(t + 1)
             nc.scalar.activation(res[:, t, :], both[:], SQUARE)
+            nc.sync.dma_start(out_blocks[:, t, Q:], res[:, t, Q:])
             nc.vector.scalar_tensor_tensor(
                 res[:, t, :Q], res[:, t, Q:], c[:, t : t + 1], res[:, t, :Q], op0=MULT, op1=MULT
             )
-            nc.sync.dma_start(out_blocks[:, t, :], res[:, t, :])
+            nc.sync.dma_start(out_blocks[:, t, :Q], res[:, t, :Q])

@@ -11,6 +11,9 @@ TANH = mybir.ActivationFunctionType.Tanh
 SQUARE = mybir.ActivationFunctionType.Square
 MULT = mybir.AluOpType.mult
 
+CHUNKS = 4
+ON_SCALAR = 448
+
 
 def tile_contrastivehessiancalculator_kernel(tc, table, w1, b1, w2, offs, out):
     nc = tc.nc
@@ -22,14 +25,16 @@ def tile_contrastivehessiancalculator_kernel(tc, table, w1, b1, w2, offs, out):
         w1_sb = held.tile([P, H], BF16, name="w1_sb")
         nc.scalar.dma_start(w1_sb[:], w1)
         table_sb = held.tile([P, S], BF16, name="table_sb")
-        nc.sync.dma_start(table_sb[:, : S // 2], table[:, : S // 2])
-        nc.scalar.dma_start(table_sb[:, S // 2 :], table[:, S // 2 :])
+        width = S // CHUNKS
+        for i in range(CHUNKS):
+            queue = nc.sync if i % 2 == 0 else nc.scalar
+            queue.dma_start(table_sb[:, i * width : (i + 1) * width], table[:, i * width : (i + 1) * width])
         offsets = held.tile([P, N // 16], U16, name="offsets")
         nc.sync.dma_start(offsets[:], offs)
         b1_sb = held.tile([P, T], F32, name="b1_sb")
         nc.sync.dma_start(b1_sb[:], b1.rearrange("(p t) o -> p (t o)", t=T))
         w2_sb = held.tile([P, T, O], F32, name="w2_sb")
-        nc.gpsimd.dma_start(w2_sb[:], w2.rearrange("(p t) o -> p t o", t=T))
+        nc.sync.dma_start(w2_sb[:], w2.rearrange("(p t) o -> p t o", t=T))
         out_blocks = out.rearrange("(p t) n -> p t n", t=T)
 
         zero = held.tile([P, 1], F32, name="zero")
@@ -38,7 +43,8 @@ def tile_contrastivehessiancalculator_kernel(tc, table, w1, b1, w2, offs, out):
         nc.scalar.activation(tanh_of_zero[:], zero[:], TANH)
 
         w1_blocks = held.tile([P, T, P], BF16, name="w1_blocks")
-        nc.vector.tensor_copy(w1_blocks[:], w1_sb[:].rearrange("k (p t) -> k t p", t=T))
+        for t in range(T):
+            nc.vector.tensor_copy(w1_blocks[:, t, :], w1_sb[:].rearrange("k (p t) -> k t p", t=T)[:, t, :])
 
         w2_sq = held.tile([P, T, O], F32, name="w2_sq")
         nc.vector.tensor_mul(w2_sq[:], w2_sb[:], w2_sb[:])
@@ -55,6 +61,7 @@ def tile_contrastivehessiancalculator_kernel(tc, table, w1, b1, w2, offs, out):
             both = work.tile([P, N], F32, name="both")
             nc.vector.tensor_add(both[:, :Q], h[:, :Q], h[:, Q:])
             nc.vector.tensor_sub(both[:, Q:], h[:, :Q], h[:, Q:])
+            nc.vector.tensor_mul(res[:, t, ON_SCALAR:], both[:, ON_SCALAR:], both[:, ON_SCALAR:])
             return both
 
         both_next = sums_and_differences(0)
@@ -62,7 +69,7 @@ def tile_contrastivehessiancalculator_kernel(tc, table, w1, b1, w2, offs, out):
             both = both_next
             if t + 1 < T:
                 both_next = sums_and_differences(t + 1)
-            nc.scalar.activation(res[:, t, :], both[:], SQUARE)
+            nc.scalar.activation(res[:, t, :ON_SCALAR], both[:, :ON_SCALAR], SQUARE)
             nc.sync.dma_start(out_blocks[:, t, Q:], res[:, t, Q:])
             nc.vector.scalar_tensor_tensor(
                 res[:, t, :Q], res[:, t, Q:], c[:, t : t + 1], res[:, t, :Q], op0=MULT, op1=MULT

@@ -11,8 +11,7 @@ TANH = mybir.ActivationFunctionType.Tanh
 SQUARE = mybir.ActivationFunctionType.Square
 MULT = mybir.AluOpType.mult
 
-CHUNKS = 4
-ON_SCALAR = 448
+AHEAD = 2
 
 
 def tile_contrastivehessiancalculator_kernel(tc, table, w1, b1, w2, offs, out):
@@ -25,16 +24,14 @@ def tile_contrastivehessiancalculator_kernel(tc, table, w1, b1, w2, offs, out):
         w1_sb = held.tile([P, H], BF16, name="w1_sb")
         nc.scalar.dma_start(w1_sb[:], w1)
         table_sb = held.tile([P, S], BF16, name="table_sb")
-        width = S // CHUNKS
-        for i in range(CHUNKS):
-            queue = nc.sync if i % 2 == 0 else nc.scalar
-            queue.dma_start(table_sb[:, i * width : (i + 1) * width], table[:, i * width : (i + 1) * width])
+        nc.sync.dma_start(table_sb[:, : S // 2], table[:, : S // 2])
+        nc.scalar.dma_start(table_sb[:, S // 2 :], table[:, S // 2 :])
         offsets = held.tile([P, N // 16], U16, name="offsets")
         nc.sync.dma_start(offsets[:], offs)
         b1_sb = held.tile([P, T], F32, name="b1_sb")
         nc.sync.dma_start(b1_sb[:], b1.rearrange("(p t) o -> p (t o)", t=T))
         w2_sb = held.tile([P, T, O], F32, name="w2_sb")
-        nc.sync.dma_start(w2_sb[:], w2.rearrange("(p t) o -> p t o", t=T))
+        nc.gpsimd.dma_start(w2_sb[:], w2.rearrange("(p t) o -> p t o", t=T))
         out_blocks = out.rearrange("(p t) n -> p t n", t=T)
 
         zero = held.tile([P, 1], F32, name="zero")
@@ -43,15 +40,7 @@ def tile_contrastivehessiancalculator_kernel(tc, table, w1, b1, w2, offs, out):
         nc.scalar.activation(tanh_of_zero[:], zero[:], TANH)
 
         w1_blocks = held.tile([P, T, P], BF16, name="w1_blocks")
-        for t in range(T):
-            nc.vector.tensor_copy(w1_blocks[:, t, :], w1_sb[:].rearrange("k (p t) -> k t p", t=T)[:, t, :])
-
-        w2_sq = held.tile([P, T, O], F32, name="w2_sq")
-        nc.vector.tensor_mul(w2_sq[:], w2_sb[:], w2_sb[:])
-        c = held.tile([P, T], F32, name="c")
-        nc.vector.reduce_sum(c[:], w2_sq[:], axis=mybir.AxisListType.X)
-
-        res = held.tile([P, T, N], F32, name="res")
+        nc.vector.tensor_copy(w1_blocks[:], w1_sb[:].rearrange("k (p t) -> k t p", t=T))
 
         def sums_and_differences(t):
             z = psum.tile([P, N], F32, name="z")
@@ -61,15 +50,20 @@ def tile_contrastivehessiancalculator_kernel(tc, table, w1, b1, w2, offs, out):
             both = work.tile([P, N], F32, name="both")
             nc.vector.tensor_add(both[:, :Q], h[:, :Q], h[:, Q:])
             nc.vector.tensor_sub(both[:, Q:], h[:, :Q], h[:, Q:])
-            nc.vector.tensor_mul(res[:, t, ON_SCALAR:], both[:, ON_SCALAR:], both[:, ON_SCALAR:])
             return both
 
-        both_next = sums_and_differences(0)
+        boths = [sums_and_differences(t) for t in range(AHEAD)]
+
+        w2_sq = held.tile([P, T, O], F32, name="w2_sq")
+        nc.vector.tensor_mul(w2_sq[:], w2_sb[:], w2_sb[:])
+        c = held.tile([P, T], F32, name="c")
+        nc.vector.reduce_sum(c[:], w2_sq[:], axis=mybir.AxisListType.X)
+
+        res = held.tile([P, T, N], F32, name="res")
         for t in range(T):
-            both = both_next
-            if t + 1 < T:
-                both_next = sums_and_differences(t + 1)
-            nc.scalar.activation(res[:, t, :ON_SCALAR], both[:, :ON_SCALAR], SQUARE)
+            if t + AHEAD < T:
+                boths.append(sums_and_differences(t + AHEAD))
+            nc.scalar.activation(res[:, t, :], boths[t][:], SQUARE)
             nc.sync.dma_start(out_blocks[:, t, Q:], res[:, t, Q:])
             nc.vector.scalar_tensor_tensor(
                 res[:, t, :Q], res[:, t, Q:], c[:, t : t + 1], res[:, t, :Q], op0=MULT, op1=MULT

@@ -3,6 +3,8 @@ import concourse.mybir as mybir
 P = 128
 D, S, H, O, N, Q = 128, 2048, 512, 64, 512, 256
 T = H // P
+G = 128
+UNITS = [(t, g) for t in range(T) for g in range(Q // G)]
 
 FLOPS = 2 * D * H * N
 
@@ -18,8 +20,8 @@ def tile_contrastivehessiancalculator_kernel(tc, table, w1, b1, w2, offs, out):
     nc = tc.nc
     with (
         tc.tile_pool(name="held", bufs=1) as held,
-        tc.tile_pool(name="work", bufs=T) as work,
-        tc.psum_pool(name="psum", bufs=T) as psum,
+        tc.tile_pool(name="work", bufs=len(UNITS)) as work,
+        tc.psum_pool(name="psum", bufs=len(UNITS)) as psum,
     ):
         w1_sb = held.tile([P, H], BF16, name="w1_sb")
         nc.scalar.dma_start(w1_sb[:], w1)
@@ -42,30 +44,33 @@ def tile_contrastivehessiancalculator_kernel(tc, table, w1, b1, w2, offs, out):
         w1_blocks = held.tile([P, T, P], BF16, name="w1_blocks")
         nc.vector.tensor_copy(w1_blocks[:], w1_sb[:].rearrange("k (p t) -> k t p", t=T))
 
-        def sums_and_differences(t):
+        def sums_and_differences(t, g):
             z = psum.tile([P, N], F32, name="z")
-            nc.tensor.matmul(z[:], w1_blocks[:, t, :], table_sb[:].indirect(offsets[:]), start=True, stop=True)
-            h = work.tile([P, N], F32, name="h")
-            nc.scalar.activation(h[:], z[:], TANH, bias=b1_sb[:, t : t + 1])
-            both = work.tile([P, N], F32, name="both")
-            nc.vector.tensor_add(both[:, :Q], h[:, :Q], h[:, Q:])
-            nc.vector.tensor_sub(both[:, Q:], h[:, :Q], h[:, Q:])
+            for side in range(2):
+                first = (side * Q + g * G) // 16
+                looked_up = table_sb[:].indirect(offsets[:, first : first + G // 16])
+                nc.tensor.matmul(
+                    z[:, side * G : (side + 1) * G], w1_blocks[:, t, :], looked_up, start=True, stop=True
+                )
+            h = work.tile([P, 2 * G], F32, name="h")
+            nc.scalar.activation(h[:], z[:, : 2 * G], TANH, bias=b1_sb[:, t : t + 1])
+            both = work.tile([P, 2 * G], F32, name="both")
+            nc.vector.tensor_add(both[:, :G], h[:, :G], h[:, G:])
+            nc.vector.tensor_sub(both[:, G:], h[:, :G], h[:, G:])
             return both
 
-        boths = [sums_and_differences(t) for t in range(AHEAD)]
+        boths = [sums_and_differences(t, g) for t, g in UNITS[:AHEAD]]
 
         w2_sq = held.tile([P, T, O], F32, name="w2_sq")
         nc.vector.tensor_mul(w2_sq[:], w2_sb[:], w2_sb[:])
         c = held.tile([P, T], F32, name="c")
         nc.vector.reduce_sum(c[:], w2_sq[:], axis=mybir.AxisListType.X)
 
-        res = held.tile([P, T, N], F32, name="res")
-        for t in range(T):
-            if t + AHEAD < T:
-                boths.append(sums_and_differences(t + AHEAD))
-            nc.scalar.activation(res[:, t, :], boths[t][:], SQUARE)
-            nc.sync.dma_start(out_blocks[:, t, Q:], res[:, t, Q:])
-            nc.vector.scalar_tensor_tensor(
-                res[:, t, :Q], res[:, t, Q:], c[:, t : t + 1], res[:, t, :Q], op0=MULT, op1=MULT
-            )
-            nc.sync.dma_start(out_blocks[:, t, :Q], res[:, t, :Q])
+        for i, (t, g) in enumerate(UNITS):
+            if i + AHEAD < len(UNITS):
+                boths.append(sums_and_differences(*UNITS[i + AHEAD]))
+            res = work.tile([P, 2 * G], F32, name="res")
+            nc.scalar.activation(res[:], boths[i][:], SQUARE)
+            nc.sync.dma_start(out_blocks[:, t, Q + g * G : Q + (g + 1) * G], res[:, G:])
+            nc.vector.scalar_tensor_tensor(res[:, :G], res[:, G:], c[:, t : t + 1], res[:, :G], op0=MULT, op1=MULT)
+            nc.sync.dma_start(out_blocks[:, t, g * G : (g + 1) * G], res[:, :G])

@@ -33,7 +33,7 @@ def tile_contrastivehessiancalculator_kernel(tc, table, w1, b1, w2, offs, out):
         b1_sb = held.tile([P, T], F32, name="b1_sb")
         nc.sync.dma_start(b1_sb[:], b1.rearrange("(p t) o -> p (t o)", t=T))
         w2_sb = held.tile([P, T, O], F32, name="w2_sb")
-        nc.gpsimd.dma_start(w2_sb[:], w2.rearrange("(p t) o -> p t o", t=T))
+        nc.scalar.dma_start(w2_sb[:], w2.rearrange("(p t) o -> p t o", t=T))
         out_blocks = out.rearrange("(p t) n -> p t n", t=T)
 
         zero = held.tile([P, 1], F32, name="zero")
@@ -43,6 +43,11 @@ def tile_contrastivehessiancalculator_kernel(tc, table, w1, b1, w2, offs, out):
 
         w1_blocks = held.tile([P, T, P], BF16, name="w1_blocks")
         nc.vector.tensor_copy(w1_blocks[:], w1_sb[:].rearrange("k (p t) -> k t p", t=T))
+
+        w2_sq = held.tile([P, T, O], F32, name="w2_sq")
+        nc.vector.tensor_mul(w2_sq[:], w2_sb[:], w2_sb[:])
+        c = held.tile([P, T], F32, name="c")
+        nc.vector.reduce_sum(c[:], w2_sq[:], axis=mybir.AxisListType.X)
 
         def sums_and_differences(t, g):
             z = psum.tile([P, N], F32, name="z")
@@ -60,11 +65,6 @@ def tile_contrastivehessiancalculator_kernel(tc, table, w1, b1, w2, offs, out):
             return both
 
         boths = [sums_and_differences(t, g) for t, g in UNITS[:AHEAD]]
-
-        w2_sq = held.tile([P, T, O], F32, name="w2_sq")
-        nc.vector.tensor_mul(w2_sq[:], w2_sb[:], w2_sb[:])
-        c = held.tile([P, T], F32, name="c")
-        nc.vector.reduce_sum(c[:], w2_sq[:], axis=mybir.AxisListType.X)
 
         for i, (t, g) in enumerate(UNITS):
             if i + AHEAD < len(UNITS):

@@ -26,8 +26,10 @@ def tile_contrastivehessiancalculator_kernel(tc, table, w1, b1, w2, offs, out):
         w1_sb = held.tile([P, H], BF16, name="w1_sb")
         nc.scalar.dma_start(w1_sb[:], w1)
         table_sb = held.tile([P, S], BF16, name="table_sb")
-        nc.sync.dma_start(table_sb[:, : S // 2], table[:, : S // 2])
-        nc.scalar.dma_start(table_sb[:, S // 2 :], table[:, S // 2 :])
+        for piece in range(4):
+            queue = nc.sync if piece % 2 == 0 else nc.scalar
+            columns = slice(piece * (S // 4), (piece + 1) * (S // 4))
+            queue.dma_start(table_sb[:, columns], table[:, columns])
         offsets = held.tile([P, N // 16], U16, name="offsets")
         nc.sync.dma_start(offsets[:], offs)
         b1_sb = held.tile([P, T], F32, name="b1_sb")

@@ -68,11 +68,15 @@ def tile_contrastivehessiancalculator_kernel(tc, table, w1, b1, w2, offs, out):
 
         boths = [sums_and_differences(t, g) for t, g in UNITS[:AHEAD]]
 
+        res = held.tile([P, T, 2, Q], F32, name="res")
         for i, (t, g) in enumerate(UNITS):
             if i + AHEAD < len(UNITS):
                 boths.append(sums_and_differences(*UNITS[i + AHEAD]))
-            res = work.tile([P, 2 * G], F32, name="res")
-            nc.scalar.activation(res[:], boths[i][:], SQUARE)
-            nc.sync.dma_start(out_blocks[:, t, Q + g * G : Q + (g + 1) * G], res[:, G:])
-            nc.vector.scalar_tensor_tensor(res[:, :G], res[:, G:], c[:, t : t + 1], res[:, :G], op0=MULT, op1=MULT)
-            nc.sync.dma_start(out_blocks[:, t, g * G : (g + 1) * G], res[:, :G])
+            pairs = slice(g * G, (g + 1) * G)
+            nc.scalar.activation(res[:, t, :, pairs], boths[i][:].rearrange("p (half q) -> p half q", half=2), SQUARE)
+            nc.vector.scalar_tensor_tensor(
+                res[:, t, 0, pairs], res[:, t, 1, pairs], c[:, t : t + 1], res[:, t, 0, pairs], op0=MULT, op1=MULT
+            )
+            if g == Q // G - 1:
+                nc.sync.dma_start(out_blocks[:, t, Q:], res[:, t, 1, :])
+                nc.sync.dma_start(out_blocks[:, t, :Q], res[:, t, 0, :])

@@ -16,6 +16,10 @@ MULT = mybir.AluOpType.mult
 AHEAD = 2
 
 
+def vector_squares_differences(i):
+    return UNITS[i][0] == 1
+
+
 def tile_contrastivehessiancalculator_kernel(tc, table, w1, b1, w2, offs, out):
     nc = tc.nc
     with (
@@ -51,7 +55,10 @@ def tile_contrastivehessiancalculator_kernel(tc, table, w1, b1, w2, offs, out):
         c = held.tile([P, T], F32, name="c")
         nc.vector.reduce_sum(c[:], w2_sq[:], axis=mybir.AxisListType.X)
 
-        def sums_and_differences(t, g):
+        res = held.tile([P, T, 2, Q], F32, name="res")
+
+        def sums_and_differences(i):
+            t, g = UNITS[i]
             z = psum.tile([P, N], F32, name="z")
             for side in range(2):
                 first = (side * Q + g * G) // 16
@@ -64,16 +71,22 @@ def tile_contrastivehessiancalculator_kernel(tc, table, w1, b1, w2, offs, out):
             both = work.tile([P, 2 * G], F32, name="both")
             nc.vector.tensor_add(both[:, :G], h[:, :G], h[:, G:])
             nc.vector.tensor_sub(both[:, G:], h[:, :G], h[:, G:])
+            if vector_squares_differences(i):
+                nc.vector.tensor_mul(res[:, t, 1, g * G : (g + 1) * G], both[:, G:], both[:, G:])
             return both
 
-        boths = [sums_and_differences(t, g) for t, g in UNITS[:AHEAD]]
+        boths = [sums_and_differences(i) for i in range(AHEAD)]
 
-        res = held.tile([P, T, 2, Q], F32, name="res")
         for i, (t, g) in enumerate(UNITS):
             if i + AHEAD < len(UNITS):
-                boths.append(sums_and_differences(*UNITS[i + AHEAD]))
+                boths.append(sums_and_differences(i + AHEAD))
             pairs = slice(g * G, (g + 1) * G)
-            nc.scalar.activation(res[:, t, :, pairs], boths[i][:].rearrange("p (half q) -> p half q", half=2), SQUARE)
+            if vector_squares_differences(i):
+                nc.scalar.activation(res[:, t, 0, pairs], boths[i][:, :G], SQUARE)
+            else:
+                nc.scalar.activation(
+                    res[:, t, :, pairs], boths[i][:].rearrange("p (half q) -> p half q", half=2), SQUARE
+                )
             nc.vector.scalar_tensor_tensor(
                 res[:, t, 0, pairs], res[:, t, 1, pairs], c[:, t : t + 1], res[:, t, 0, pairs], op0=MULT, op1=MULT
             )

@@ -20,6 +20,10 @@ def vector_squares_differences(i):
     return UNITS[i][0] == 1
 
 
+def vector_squares_products(i):
+    return UNITS[i][0] == T - 1
+
+
 def tile_contrastivehessiancalculator_kernel(tc, table, w1, b1, w2, offs, out):
     nc = tc.nc
     with (
@@ -69,8 +73,8 @@ def tile_contrastivehessiancalculator_kernel(tc, table, w1, b1, w2, offs, out):
             h = work.tile([P, 2 * G], F32, name="h")
             nc.scalar.activation(h[:], z[:, : 2 * G], TANH, bias=b1_sb[:, t : t + 1])
             both = work.tile([P, 2 * G], F32, name="both")
-            nc.vector.tensor_add(both[:, :G], h[:, :G], h[:, G:])
             nc.vector.tensor_sub(both[:, G:], h[:, :G], h[:, G:])
+            nc.vector.tensor_add(both[:, :G], h[:, :G], h[:, G:])
             if vector_squares_differences(i):
                 nc.vector.tensor_mul(res[:, t, 1, g * G : (g + 1) * G], both[:, G:], both[:, G:])
             return both
@@ -81,15 +85,24 @@ def tile_contrastivehessiancalculator_kernel(tc, table, w1, b1, w2, offs, out):
             if i + AHEAD < len(UNITS):
                 boths.append(sums_and_differences(i + AHEAD))
             pairs = slice(g * G, (g + 1) * G)
-            if vector_squares_differences(i):
-                nc.scalar.activation(res[:, t, 0, pairs], boths[i][:, :G], SQUARE)
-            else:
-                nc.scalar.activation(
-                    res[:, t, :, pairs], boths[i][:].rearrange("p (half q) -> p half q", half=2), SQUARE
+            sums, differences = boths[i][:, :G], boths[i][:, G:]
+            if vector_squares_products(i):
+                nc.scalar.activation(res[:, t, 1, pairs], differences, SQUARE)
+                product = work.tile([P, G], F32, name="product")
+                nc.vector.tensor_mul(product[:], sums, differences)
+                nc.vector.scalar_tensor_tensor(
+                    res[:, t, 0, pairs], product[:], c[:, t : t + 1], product[:], op0=MULT, op1=MULT
                 )
-            nc.vector.scalar_tensor_tensor(
-                res[:, t, 0, pairs], res[:, t, 1, pairs], c[:, t : t + 1], res[:, t, 0, pairs], op0=MULT, op1=MULT
-            )
+            else:
+                if vector_squares_differences(i):
+                    nc.scalar.activation(res[:, t, 0, pairs], sums, SQUARE)
+                else:
+                    nc.scalar.activation(
+                        res[:, t, :, pairs], boths[i][:].rearrange("p (half q) -> p half q", half=2), SQUARE
+                    )
+                nc.vector.scalar_tensor_tensor(
+                    res[:, t, 0, pairs], res[:, t, 1, pairs], c[:, t : t + 1], res[:, t, 0, pairs], op0=MULT, op1=MULT
+                )
             if g == Q // G - 1:
                 nc.sync.dma_start(out_blocks[:, t, Q:], res[:, t, 1, :])
                 nc.sync.dma_start(out_blocks[:, t, :Q], res[:, t, 0, :])

import concourse.mybir as mybir

P = 128
D, S, H, O, N, Q = 128, 2048, 512, 64, 512, 256
T = H // P
G = 128
UNITS = [(t, g) for t in range(T) for g in range(Q // G)]

FLOPS = 2 * D * H * N

BF16, F32, U16 = mybir.dt.bfloat16, mybir.dt.float32, mybir.dt.uint16
TANH = mybir.ActivationFunctionType.Tanh
SQUARE = mybir.ActivationFunctionType.Square
MULT = mybir.AluOpType.mult

AHEAD = 2


def vector_squares_differences(i):
    return UNITS[i][0] == 1


def vector_squares_products(i):
    return UNITS[i][0] == T - 1


def tile_contrastivehessiancalculator_kernel(tc, table, w1, b1, w2, offs, out):
    nc = tc.nc
    with (
        tc.tile_pool(name="held", bufs=1) as held,
        tc.tile_pool(name="work", bufs=len(UNITS)) as work,
        tc.psum_pool(name="psum", bufs=len(UNITS)) as psum,
    ):
        w1_sb = held.tile([P, H], BF16, name="w1_sb")
        nc.scalar.dma_start(w1_sb[:], w1)
        table_sb = held.tile([P, S], BF16, name="table_sb")
        for piece in range(4):
            queue = nc.sync if piece % 2 == 0 else nc.scalar
            columns = slice(piece * (S // 4), (piece + 1) * (S // 4))
            queue.dma_start(table_sb[:, columns], table[:, columns])
        offsets = held.tile([P, N // 16], U16, name="offsets")
        nc.sync.dma_start(offsets[:], offs)
        b1_sb = held.tile([P, T], F32, name="b1_sb")
        nc.sync.dma_start(b1_sb[:], b1.rearrange("(p t) o -> p (t o)", t=T))
        w2_sb = held.tile([P, T, O], F32, name="w2_sb")
        nc.scalar.dma_start(w2_sb[:], w2.rearrange("(p t) o -> p t o", t=T))
        out_blocks = out.rearrange("(p t) n -> p t n", t=T)

        zero = held.tile([P, 1], F32, name="zero")
        nc.vector.memset(zero[:], 0.0)
        tanh_of_zero = held.tile([P, 1], F32, name="tanh_of_zero")
        nc.scalar.activation(tanh_of_zero[:], zero[:], TANH)

        w1_blocks = held.tile([P, T, P], BF16, name="w1_blocks")
        nc.vector.tensor_copy(w1_blocks[:], w1_sb[:].rearrange("k (p t) -> k t p", t=T))

        w2_sq = held.tile([P, T, O], F32, name="w2_sq")
        nc.vector.tensor_mul(w2_sq[:], w2_sb[:], w2_sb[:])
        c = held.tile([P, T], F32, name="c")
        nc.vector.reduce_sum(c[:], w2_sq[:], axis=mybir.AxisListType.X)

        res = held.tile([P, T, 2, Q], F32, name="res")

        def sums_and_differences(i):
            t, g = UNITS[i]
            z = psum.tile([P, N], F32, name="z")
            for side in range(2):
                first = (side * Q + g * G) // 16
                looked_up = table_sb[:].indirect(offsets[:, first : first + G // 16])
                nc.tensor.matmul(
                    z[:, side * G : (side + 1) * G], w1_blocks[:, t, :], looked_up, start=True, stop=True
                )
            h = work.tile([P, 2 * G], F32, name="h")
            nc.scalar.activation(h[:], z[:, : 2 * G], TANH, bias=b1_sb[:, t : t + 1])
            both = work.tile([P, 2 * G], F32, name="both")
            nc.vector.tensor_sub(both[:, G:], h[:, :G], h[:, G:])
            nc.vector.tensor_add(both[:, :G], h[:, :G], h[:, G:])
            if vector_squares_differences(i):
                nc.vector.tensor_mul(res[:, t, 1, g * G : (g + 1) * G], both[:, G:], both[:, G:])
            return both

        boths = [sums_and_differences(i) for i in range(AHEAD)]

        for i, (t, g) in enumerate(UNITS):
            if i + AHEAD < len(UNITS):
                boths.append(sums_and_differences(i + AHEAD))
            pairs = slice(g * G, (g + 1) * G)
            sums, differences = boths[i][:, :G], boths[i][:, G:]
            if vector_squares_products(i):
                nc.scalar.activation(res[:, t, 1, pairs], differences, SQUARE)
                product = work.tile([P, G], F32, name="product")
                nc.vector.tensor_mul(product[:], sums, differences)
                nc.vector.scalar_tensor_tensor(
                    res[:, t, 0, pairs], product[:], c[:, t : t + 1], product[:], op0=MULT, op1=MULT
                )
            else:
                if vector_squares_differences(i):
                    nc.scalar.activation(res[:, t, 0, pairs], sums, SQUARE)
                else:
                    nc.scalar.activation(
                        res[:, t, :, pairs], boths[i][:].rearrange("p (half q) -> p half q", half=2), SQUARE
                    )
                nc.vector.scalar_tensor_tensor(
                    res[:, t, 0, pairs], res[:, t, 1, pairs], c[:, t : t + 1], res[:, t, 0, pairs], op0=MULT, op1=MULT
                )
            if g == Q // G - 1:
                nc.sync.dma_start(out_blocks[:, t, Q:], res[:, t, 1, :])
                nc.sync.dma_start(out_blocks[:, t, :Q], res[:, t, 0, :])
